import numpy as np
import ml_dtypes


def mxq(x, axis, fmt="e4m3"):
    dtype, down = {"e4m3": (ml_dtypes.float8_e4m3fn, 7), "e5m2": (ml_dtypes.float8_e5m2, 14)}[fmt]
    v = np.moveaxis(np.asarray(x, np.float32).astype(ml_dtypes.bfloat16).astype(np.float64), axis, -1)
    blocks = v.reshape(v.shape[:-1] + (-1, 32))
    amax = np.abs(blocks).max(-1, keepdims=True)
    byte = np.maximum(np.where(amax > 0, np.frexp(amax)[1] - 1 + 127, 0) - down, 1)
    scale = np.exp2(byte - 127.0)
    codes = (blocks / scale).astype(np.float32).astype(dtype).astype(np.float64)
    return np.moveaxis((codes * scale).reshape(v.shape), -1, axis)


WIDE = False


def mx_kscale(k):
    if not WIDE:
        return np.ones(k)
    levels = np.array([10, -10, 5, -5, 0])
    a = np.random.permutation(np.resize(levels, k // 512 * 4)).reshape(k // 512, 4)
    idx = np.arange(k)
    return np.exp2(a[idx // 512, idx % 128 // 32])


BF16 = ml_dtypes.bfloat16


def bf(x):
    return np.asarray(x, np.float32).astype(BF16)


def f64(x):
    return np.asarray(x).astype(np.float64)


N, T, C, D, H, DO = 8, 1024, 1024, 256, 16, 1024
HD = D // H


def head_scores(q, k):
    return np.stack([(q * k[:, :, g:g + 1, :]).sum(-1) for g in range(H)], axis=-1)


def setup_inputs():
    s = mx_kscale(C)
    return {"x": bf(np.random.standard_normal((N, T, C)) * s),
            "w_qk": bf(np.random.standard_normal((C, 2 * D)) / np.sqrt(C) / s[:, None]),
            "b_qk": bf(np.random.standard_normal(2 * D) * 0.3)}


def reference(x, w_qk, b_qk):
    qk = (mxq(f64(x), 2, "e4m3") @ mxq(f64(w_qk), 0, "e4m3")) + f64(b_qk)
    qk = qk.reshape(N, T, 2, H, HD)
    q, k = qk[:, :, 0], qk[:, :, 1]
    s = head_scores(q * HD ** -0.5, k)
    e = np.exp(s - s.max(-1, keepdims=True))
    return e / e.sum(-1, keepdims=True)

@@ -1,0 +1,288 @@
+from contextlib import ExitStack
+
+import concourse.mybir as mybir
+from concourse.masks import make_identity
+
+F32 = mybir.dt.float32
+BF16 = mybir.dt.bfloat16
+U32 = mybir.dt.uint32
+U8 = mybir.dt.uint8
+FP8X4 = mybir.dt.float8_e4m3fn_x4
+ALU = mybir.AluOpType
+ACT = mybir.ActivationFunctionType
+AXIS = mybir.AxisListType
+
+P = 128
+BATCH = 8
+TOKENS = 1024
+K = 1024
+HEADS = 16
+HD = 16
+QK_HEADS = 2 * HEADS
+QK_COLS = QK_HEADS * HD
+PACK = 4
+PASSES = K // (P * PACK)
+WORD_TILES = K // 2 // P
+SLOTS = TOKENS // P
+
+QUARTERS = 4
+UNITS = BATCH * QUARTERS
+TILES_PER_UNIT = SLOTS // QUARTERS
+HEADS_PER_BANK = 4
+BANKS_PER_UNIT = QK_HEADS // HEADS_PER_BANK // QUARTERS
+GROUPS_PER_UNIT = P // QUARTERS
+
+LOAD_AHEAD = 3
+PROJECT_LAG = 1
+TURN_LAG = QUARTERS
+KEEP_LAG = TURN_LAG + 1
+SPREAD_LAG = KEEP_LAG + 2
+SCORE_LAG = KEEP_LAG + QUARTERS - 1
+SOFTMAX_LAG = SCORE_LAG + 1
+
+SPREAD_ON_SCALAR = 3
+
+FLOPS = 2 * BATCH * TOKENS * K * QK_COLS + 2 * BATCH * TOKENS * HEADS * HEADS * HD
+
+
+def tile_attention_pa_t_kernel(tc, x, w_qk, b_qk, out):
+    nc = tc.nc
+    with ExitStack() as stack:
+        stack.enter_context(tc.manual_schedule())
+        const = stack.enter_context(tc.tile_pool(name="const", bufs=1))
+        w_stage = stack.enter_context(tc.tile_pool(name="w_stage", bufs=1))
+        x_pool = stack.enter_context(tc.tile_pool(name="x_pool", bufs=LOAD_AHEAD + 1))
+        mx_pool = stack.enter_context(tc.tile_pool(name="mx_pool", bufs=2))
+        batch_pool = stack.enter_context(tc.tile_pool(name="batch_pool", bufs=2))
+        block_pool = stack.enter_context(tc.tile_pool(name="block_pool", bufs=2))
+        soft_pool = stack.enter_context(tc.tile_pool(name="soft_pool", bufs=3))
+        psum_xt = stack.enter_context(tc.psum_pool(name="psum_xt", bufs=2))
+        psum_qk = stack.enter_context(tc.psum_pool(name="psum_qk", bufs=2))
+        psum_turn = stack.enter_context(tc.psum_pool(name="psum_turn", bufs=2))
+        psum_score = stack.enter_context(tc.psum_pool(name="psum_score", bufs=2))
+
+        x_pairs = {}
+        x_grouped_of = {}
+        x_mx_of = {}
+        qk_rows_of = {}
+        turned_of = {}
+        qk_turned_of = {}
+        q_blocks_of = {}
+        score_of = {}
+        prob_of = {}
+
+        def load_x(unit):
+            n, quarter = divmod(unit, QUARTERS)
+            j0 = quarter * TILES_PER_UNIT
+            x_pair = x_pool.tile([P, TILES_PER_UNIT, K], BF16)
+            nc.sync.dma_start(
+                out=x_pair[:],
+                in_=x[n].rearrange("(t j) k -> t j k", j=SLOTS)[:, j0 : j0 + TILES_PER_UNIT, :],
+            )
+            x_pairs[unit] = x_pair
+
+        for unit in range(LOAD_AHEAD):
+            load_x(unit)
+
+        ident = const.tile([P, P], F32)
+        make_identity(nc, ident[:])
+        slot_of_partition = const.tile([P, SLOTS], F32)
+        nc.vector.tensor_reduce(
+            out=slot_of_partition[:],
+            in_=ident[:].rearrange("p (j d) -> p j d", d=HD),
+            axis=AXIS.X,
+            op=ALU.add,
+        )
+        slot_mask = const.tile([P, SLOTS], F32)
+        nc.vector.tensor_scalar(
+            out=slot_mask[:], in0=slot_of_partition[:], scalar1=HD**-0.5, scalar2=None, op0=ALU.mult
+        )
+
+        w_codes = const.tile([P, PASSES, QK_COLS], U32, align_bytes=64)
+        w_scales = const.tile([P, PASSES, QK_COLS], U8, align_bytes=64)
+        for c in range(PASSES):
+            w_rows = w_stage.tile([P, PACK, QK_COLS], BF16, name="w_rows%d" % c)
+            for u in range(2):
+                first = (2 * c + u) * 2 * P
+                nc.sync.dma_start(
+                    out=w_rows[:, 2 * u : 2 * u + 2, :],
+                    in_=w_qk[first : first + 2 * P, :].rearrange("(p e) n -> p e n", e=2),
+                )
+            w_grouped = w_stage.tile([P, QK_COLS, PACK], BF16, align_bytes=64, name="w_grouped%d" % c)
+            nc.vector.tensor_copy(out=w_grouped[:], in_=w_rows[:].rearrange("p v n -> p n v"))
+            nc.vector.quantize_mx(
+                out=w_codes[:, c, :].bitcast(FP8X4),
+                scales=w_scales[:, c, :],
+                in_=w_grouped[:].rearrange("p n v -> p (n v)"),
+            )
+
+        bias_bf16 = const.tile([P, QK_COLS], BF16)
+        nc.sync.dma_start(out=bias_bf16[:], in_=b_qk.partition_broadcast(P))
+        bias = const.tile([P, QK_COLS], F32)
+        nc.vector.tensor_copy(out=bias[:], in_=bias_bf16[:])
+
+        def turn_x(unit):
+            x_grouped = mx_pool.tile([P, TILES_PER_UNIT, K], BF16, align_bytes=64)
+            for i in range(TILES_PER_UNIT):
+                x_words = x_pairs[unit][:, i, :].bitcast(F32)
+                x_turned = psum_xt.tile([P, WORD_TILES, P], F32)
+                for w in range(WORD_TILES):
+                    nc.tensor.transpose(x_turned[:, w, :], x_words[:, w * P : (w + 1) * P], ident[:])
+                nc.scalar.copy(
+                    out=x_grouped[:, i, :].bitcast(F32).rearrange("p (c t u) -> p c t u", c=PASSES, u=2),
+                    in_=x_turned[:].rearrange("p (c u) t -> p c t u", u=2),
+                )
+            x_grouped_of[unit] = x_grouped
+
+        def quantise_x(unit):
+            x_codes = mx_pool.tile([P, TILES_PER_UNIT, PASSES, P], U32, align_bytes=64)
+            x_scales = mx_pool.tile([P, TILES_PER_UNIT, PASSES, P], U8, align_bytes=64)
+            nc.vector.quantize_mx(
+                out=x_codes[:].rearrange("p i c t -> p (i c t)").bitcast(FP8X4),
+                scales=x_scales[:].rearrange("p i c t -> p (i c t)"),
+                in_=x_grouped_of[unit][:].rearrange("p i k -> p (i k)"),
+            )
+            x_mx_of[unit] = (x_codes, x_scales)
+
+        def project(unit):
+            n, quarter = divmod(unit, QUARTERS)
+            if quarter == 0:
+                qk_rows = batch_pool.tile([P, QK_HEADS, SLOTS, HD], F32)
+                qk_rows_of[n] = qk_rows
+            x_codes, x_scales = x_mx_of[unit]
+            for i in range(TILES_PER_UNIT):
+                qk_sum = psum_qk.tile([P, QK_COLS], F32)
+                for c in range(PASSES):
+                    nc.tensor.matmul_mx(
+                        out=qk_sum[:],
+                        lhsT=x_codes[:, i, c, :].bitcast(FP8X4),
+                        lhsT_scale=x_scales[:, i, c, :],
+                        rhs=w_codes[:, c, :].bitcast(FP8X4),
+                        rhs_scale=w_scales[:, c, :],
+                        start=(c == 0),
+                        stop=(c == PASSES - 1),
+                    )
+                nc.vector.tensor_tensor(
+                    out=qk_rows_of[n][:, :, quarter * TILES_PER_UNIT + i, :],
+                    in0=qk_sum[:].rearrange("p (h d) -> p h d", d=HD),
+                    in1=bias[:].rearrange("p (h d) -> p h d", d=HD),
+                    op=ALU.add,
+                )
+
+        def turn_qk(unit):
+            n, quarter = divmod(unit, QUARTERS)
+            banks = []
+            for i in range(BANKS_PER_UNIT):
+                head0 = (quarter * BANKS_PER_UNIT + i) * HEADS_PER_BANK
+                turned = psum_turn.tile([P, HEADS_PER_BANK, P], F32)
+                for h in range(HEADS_PER_BANK):
+                    nc.tensor.transpose(
+                        turned[:, h, :],
+                        qk_rows_of[n][:, head0 + h, :, :].rearrange("p j d -> p (j d)"),
+                        ident[:],
+                    )
+                banks.append(turned)
+            turned_of[unit] = banks
+
+        def keep_turned(unit):
+            n, quarter = divmod(unit, QUARTERS)
+            if quarter == 0:
+                qk_turned = batch_pool.tile([P, P, QK_HEADS], F32)
+                qk_turned_of[n] = qk_turned
+            for i in range(BANKS_PER_UNIT):
+                head0 = (quarter * BANKS_PER_UNIT + i) * HEADS_PER_BANK
+                nc.scalar.copy(
+                    out=qk_turned_of[n][:, :, head0 : head0 + HEADS_PER_BANK],
+                    in_=turned_of[unit][i][:].rearrange("p h t -> p t h"),
+                )
+
+        def spread_q(unit):
+            n, quarter = divmod(unit, QUARTERS)
+            t0 = quarter * GROUPS_PER_UNIT
+            q_of_groups = qk_turned_of[n][:, t0 : t0 + GROUPS_PER_UNIT, 0:HEADS]
+            q_blocks = block_pool.tile([P, GROUPS_PER_UNIT, SLOTS, HEADS], F32)
+            for j in range(SLOTS):
+                if j < SPREAD_ON_SCALAR:
+                    nc.scalar.activation(
+                        out=q_blocks[:, :, j, :],
+                        in_=q_of_groups,
+                        func=ACT.Copy,
+                        scale=slot_mask[:, j : j + 1],
+                    )
+                else:
+                    nc.vector.tensor_scalar(
+                        out=q_blocks[:, :, j, :],
+                        in0=q_of_groups,
+                        scalar1=slot_mask[:, j : j + 1],
+                        scalar2=None,
+                        op0=ALU.mult,
+                    )
+            q_blocks_of[unit] = q_blocks
+
+        def scores(unit):
+            n, quarter = divmod(unit, QUARTERS)
+            t0 = quarter * GROUPS_PER_UNIT
+            score = psum_score.tile([P, GROUPS_PER_UNIT, HEADS], F32)
+            for i in range(GROUPS_PER_UNIT):
+                nc.tensor.matmul(
+                    out=score[:, i, :],
+                    lhsT=q_blocks_of[unit][:, i, :, :].rearrange("p j h -> p (j h)"),
+                    rhs=qk_turned_of[n][:, t0 + i, HEADS:QK_HEADS],
+                    start=True,
+                    stop=True,
+                )
+            score_of[unit] = score
+
+        def subtract_top(unit):
+            score = score_of[unit]
+            top = soft_pool.tile([P, GROUPS_PER_UNIT], F32)
+            nc.vector.tensor_reduce(out=top[:], in_=score[:], axis=AXIS.X, op=ALU.max)
+            prob = soft_pool.tile([P, GROUPS_PER_UNIT, HEADS], F32)
+            nc.vector.tensor_tensor(
+                out=prob[:],
+                in0=score[:],
+                in1=top[:].unsqueeze(2).to_broadcast([P, GROUPS_PER_UNIT, HEADS]),
+                op=ALU.subtract,
+            )
+            prob_of[unit] = prob
+
+        def exponential(unit):
+            nc.scalar.activation(out=prob_of[unit][:], in_=prob_of[unit][:], func=ACT.Exp)
+
+        def normalise_and_store(unit):
+            n, quarter = divmod(unit, QUARTERS)
+            prob = prob_of[unit]
+            total = soft_pool.tile([P, GROUPS_PER_UNIT], F32)
+            nc.vector.tensor_reduce(out=total[:], in_=prob[:], axis=AXIS.X, op=ALU.add)
+            inverse = soft_pool.tile([P, GROUPS_PER_UNIT], F32)
+            nc.vector.reciprocal(out=inverse[:], in_=total[:])
+            nc.vector.tensor_tensor(
+                out=prob[:],
+                in0=prob[:],
+                in1=inverse[:].unsqueeze(2).to_broadcast([P, GROUPS_PER_UNIT, HEADS]),
+                op=ALU.mult,
+            )
+            first = quarter * GROUPS_PER_UNIT * SLOTS
+            nc.sync.dma_start(
+                out=out[n, first : first + GROUPS_PER_UNIT * SLOTS].rearrange(
+                    "(t j) h g -> (j h) t g", j=SLOTS
+                ),
+                in_=prob[:],
+            )
+
+        def run(stage, unit):
+            if 0 <= unit < UNITS:
+                stage(unit)
+
+        for step in range(UNITS + SOFTMAX_LAG):
+            run(load_x, step + LOAD_AHEAD)
+            run(keep_turned, step - KEEP_LAG)
+            run(subtract_top, step - SOFTMAX_LAG)
+            run(project, step - PROJECT_LAG)
+            run(exponential, step - SOFTMAX_LAG)
+            run(turn_x, step)
+            run(spread_q, step - SPREAD_LAG)
+            run(quantise_x, step)
+            run(scores, step - SCORE_LAG)
+            run(normalise_and_store, step - SOFTMAX_LAG)
+            run(turn_qk, step - TURN_LAG)

@@ -25,19 +25,19 @@ PASSES = K // (P * PACK)
 WORD_TILES = K // 2 // P
 SLOTS = TOKENS // P
 
-QUARTERS = 4
-UNITS = BATCH * QUARTERS
-TILES_PER_UNIT = SLOTS // QUARTERS
-HEADS_PER_BANK = 4
-BANKS_PER_UNIT = QK_HEADS // HEADS_PER_BANK // QUARTERS
-GROUPS_PER_UNIT = P // QUARTERS
+PARTS = SLOTS
+UNITS = BATCH * PARTS
+HEADS_PER_BANK = QK_HEADS // PARTS
+GROUPS_PER_UNIT = P // PARTS
+RIDE_ALONG = 8
+SCORE_COLS = RIDE_ALONG + HEADS
 
-LOAD_AHEAD = 3
+LOAD_AHEAD = 4
 PROJECT_LAG = 1
-TURN_LAG = QUARTERS
+TURN_LAG = PARTS - 1 + PROJECT_LAG
 KEEP_LAG = TURN_LAG + 1
-SPREAD_LAG = KEEP_LAG + 2
-SCORE_LAG = KEEP_LAG + QUARTERS - 1
+SCORE_LAG = KEEP_LAG + PARTS - 1
+SPREAD_LAG = SCORE_LAG - 1
 SOFTMAX_LAG = SCORE_LAG + 1
 
 SPREAD_ON_SCALAR = 3
@@ -50,7 +50,6 @@ def tile_attention_pa_t_kernel(tc, x, w_qk, b_qk, out):
     with ExitStack() as stack:
         stack.enter_context(tc.manual_schedule())
         const = stack.enter_context(tc.tile_pool(name="const", bufs=1))
-        w_stage = stack.enter_context(tc.tile_pool(name="w_stage", bufs=1))
         x_pool = stack.enter_context(tc.tile_pool(name="x_pool", bufs=LOAD_AHEAD + 1))
         mx_pool = stack.enter_context(tc.tile_pool(name="mx_pool", bufs=2))
         batch_pool = stack.enter_context(tc.tile_pool(name="batch_pool", bufs=2))
@@ -61,9 +60,10 @@ def tile_attention_pa_t_kernel(tc, x, w_qk, b_qk, out):
         psum_turn = stack.enter_context(tc.psum_pool(name="psum_turn", bufs=2))
         psum_score = stack.enter_context(tc.psum_pool(name="psum_score", bufs=2))
 
-        x_pairs = {}
+        x_rows_of = {}
         x_grouped_of = {}
         x_mx_of = {}
+        qk_sum_of = {}
         qk_rows_of = {}
         turned_of = {}
         qk_turned_of = {}
@@ -72,17 +72,12 @@ def tile_attention_pa_t_kernel(tc, x, w_qk, b_qk, out):
         prob_of = {}
 
         def load_x(unit):
-            n, quarter = divmod(unit, QUARTERS)
-            j0 = quarter * TILES_PER_UNIT
-            x_pair = x_pool.tile([P, TILES_PER_UNIT, K], BF16)
-            nc.sync.dma_start(
-                out=x_pair[:],
-                in_=x[n].rearrange("(t j) k -> t j k", j=SLOTS)[:, j0 : j0 + TILES_PER_UNIT, :],
-            )
-            x_pairs[unit] = x_pair
+            n, j = divmod(unit, PARTS)
+            x_rows = x_pool.tile([P, K], BF16)
+            nc.sync.dma_start(out=x_rows[:], in_=x[n].rearrange("(t j) k -> t j k", j=SLOTS)[:, j, :])
+            x_rows_of[unit] = x_rows
 
-        for unit in range(LOAD_AHEAD):
-            load_x(unit)
+        load_x(0)
 
         ident = const.tile([P, P], F32)
         make_identity(nc, ident[:])
@@ -101,14 +96,14 @@ def tile_attention_pa_t_kernel(tc, x, w_qk, b_qk, out):
         w_codes = const.tile([P, PASSES, QK_COLS], U32, align_bytes=64)
         w_scales = const.tile([P, PASSES, QK_COLS], U8, align_bytes=64)
         for c in range(PASSES):
-            w_rows = w_stage.tile([P, PACK, QK_COLS], BF16, name="w_rows%d" % c)
+            w_rows = const.tile([P, PACK, QK_COLS], BF16, name="w_rows%d" % c)
             for u in range(2):
                 first = (2 * c + u) * 2 * P
                 nc.sync.dma_start(
                     out=w_rows[:, 2 * u : 2 * u + 2, :],
                     in_=w_qk[first : first + 2 * P, :].rearrange("(p e) n -> p e n", e=2),
                 )
-            w_grouped = w_stage.tile([P, QK_COLS, PACK], BF16, align_bytes=64, name="w_grouped%d" % c)
+            w_grouped = const.tile([P, QK_COLS, PACK], BF16, align_bytes=64, name="w_grouped%d" % c)
             nc.vector.tensor_copy(out=w_grouped[:], in_=w_rows[:].rearrange("p v n -> p n v"))
             nc.vector.quantize_mx(
                 out=w_codes[:, c, :].bitcast(FP8X4),
@@ -121,84 +116,83 @@ def tile_attention_pa_t_kernel(tc, x, w_qk, b_qk, out):
         bias = const.tile([P, QK_COLS], F32)
         nc.vector.tensor_copy(out=bias[:], in_=bias_bf16[:])
 
+        for unit in range(1, LOAD_AHEAD):
+            load_x(unit)
+
         def turn_x(unit):
-            x_grouped = mx_pool.tile([P, TILES_PER_UNIT, K], BF16, align_bytes=64)
-            for i in range(TILES_PER_UNIT):
-                x_words = x_pairs[unit][:, i, :].bitcast(F32)
-                x_turned = psum_xt.tile([P, WORD_TILES, P], F32)
-                for w in range(WORD_TILES):
-                    nc.tensor.transpose(x_turned[:, w, :], x_words[:, w * P : (w + 1) * P], ident[:])
-                nc.scalar.copy(
-                    out=x_grouped[:, i, :].bitcast(F32).rearrange("p (c t u) -> p c t u", c=PASSES, u=2),
-                    in_=x_turned[:].rearrange("p (c u) t -> p c t u", u=2),
-                )
+            x_words = x_rows_of[unit][:].bitcast(F32)
+            x_turned = psum_xt.tile([P, WORD_TILES, P], F32)
+            for w in range(WORD_TILES):
+                nc.tensor.transpose(x_turned[:, w, :], x_words[:, w * P : (w + 1) * P], ident[:])
+            x_grouped = mx_pool.tile([P, K], BF16, align_bytes=64)
+            nc.scalar.copy(
+                out=x_grouped[:].bitcast(F32).rearrange("p (c t u) -> p c t u", c=PASSES, u=2),
+                in_=x_turned[:].rearrange("p (c u) t -> p c t u", u=2),
+            )
             x_grouped_of[unit] = x_grouped
 
         def quantise_x(unit):
-            x_codes = mx_pool.tile([P, TILES_PER_UNIT, PASSES, P], U32, align_bytes=64)
-            x_scales = mx_pool.tile([P, TILES_PER_UNIT, PASSES, P], U8, align_bytes=64)
+            x_codes = mx_pool.tile([P, PASSES, P], U32, align_bytes=64)
+            x_scales = mx_pool.tile([P, PASSES, P], U8, align_bytes=64)
             nc.vector.quantize_mx(
-                out=x_codes[:].rearrange("p i c t -> p (i c t)").bitcast(FP8X4),
-                scales=x_scales[:].rearrange("p i c t -> p (i c t)"),
-                in_=x_grouped_of[unit][:].rearrange("p i k -> p (i k)"),
+                out=x_codes[:].rearrange("p c t -> p (c t)").bitcast(FP8X4),
+                scales=x_scales[:].rearrange("p c t -> p (c t)"),
+                in_=x_grouped_of[unit][:],
             )
             x_mx_of[unit] = (x_codes, x_scales)
 
-        def project(unit):
-            n, quarter = divmod(unit, QUARTERS)
-            if quarter == 0:
+        def project_pass(unit, c):
+            if c == 0:
+                qk_sum = psum_qk.tile([P, QK_COLS], F32)
+                qk_sum_of[unit] = qk_sum
+            x_codes, x_scales = x_mx_of[unit]
+            nc.tensor.matmul_mx(
+                out=qk_sum_of[unit][:],
+                lhsT=x_codes[:, c, :].bitcast(FP8X4),
+                lhsT_scale=x_scales[:, c, :],
+                rhs=w_codes[:, c, :].bitcast(FP8X4),
+                rhs_scale=w_scales[:, c, :],
+                start=(c == 0),
+                stop=(c == PASSES - 1),
+            )
+
+        def add_bias(unit):
+            n, j = divmod(unit, PARTS)
+            if j == 0:
                 qk_rows = batch_pool.tile([P, QK_HEADS, SLOTS, HD], F32)
                 qk_rows_of[n] = qk_rows
-            x_codes, x_scales = x_mx_of[unit]
-            for i in range(TILES_PER_UNIT):
-                qk_sum = psum_qk.tile([P, QK_COLS], F32)
-                for c in range(PASSES):
-                    nc.tensor.matmul_mx(
-                        out=qk_sum[:],
-                        lhsT=x_codes[:, i, c, :].bitcast(FP8X4),
-                        lhsT_scale=x_scales[:, i, c, :],
-                        rhs=w_codes[:, c, :].bitcast(FP8X4),
-                        rhs_scale=w_scales[:, c, :],
-                        start=(c == 0),
-                        stop=(c == PASSES - 1),
-                    )
-                nc.vector.tensor_tensor(
-                    out=qk_rows_of[n][:, :, quarter * TILES_PER_UNIT + i, :],
-                    in0=qk_sum[:].rearrange("p (h d) -> p h d", d=HD),
-                    in1=bias[:].rearrange("p (h d) -> p h d", d=HD),
-                    op=ALU.add,
-                )
+            nc.vector.tensor_tensor(
+                out=qk_rows_of[n][:, :, j, :],
+                in0=qk_sum_of[unit][:].rearrange("p (h d) -> p h d", d=HD),
+                in1=bias[:].rearrange("p (h d) -> p h d", d=HD),
+                op=ALU.add,
+            )
 
         def turn_qk(unit):
-            n, quarter = divmod(unit, QUARTERS)
-            banks = []
-            for i in range(BANKS_PER_UNIT):
-                head0 = (quarter * BANKS_PER_UNIT + i) * HEADS_PER_BANK
-                turned = psum_turn.tile([P, HEADS_PER_BANK, P], F32)
-                for h in range(HEADS_PER_BANK):
-                    nc.tensor.transpose(
-                        turned[:, h, :],
-                        qk_rows_of[n][:, head0 + h, :, :].rearrange("p j d -> p (j d)"),
-                        ident[:],
-                    )
-                banks.append(turned)
-            turned_of[unit] = banks
+            n, part = divmod(unit, PARTS)
+            turned = psum_turn.tile([P, HEADS_PER_BANK, P], F32)
+            for h in range(HEADS_PER_BANK):
+                nc.tensor.transpose(
+                    turned[:, h, :],
+                    qk_rows_of[n][:, part * HEADS_PER_BANK + h, :, :].rearrange("p j d -> p (j d)"),
+                    ident[:],
+                )
+            turned_of[unit] = turned
 
         def keep_turned(unit):
-            n, quarter = divmod(unit, QUARTERS)
-            if quarter == 0:
+            n, part = divmod(unit, PARTS)
+            if part == 0:
                 qk_turned = batch_pool.tile([P, P, QK_HEADS], F32)
                 qk_turned_of[n] = qk_turned
-            for i in range(BANKS_PER_UNIT):
-                head0 = (quarter * BANKS_PER_UNIT + i) * HEADS_PER_BANK
-                nc.scalar.copy(
-                    out=qk_turned_of[n][:, :, head0 : head0 + HEADS_PER_BANK],
-                    in_=turned_of[unit][i][:].rearrange("p h t -> p t h"),
-                )
+            head0 = part * HEADS_PER_BANK
+            nc.scalar.copy(
+                out=qk_turned_of[n][:, :, head0 : head0 + HEADS_PER_BANK],
+                in_=turned_of[unit][:].rearrange("p h t -> p t h"),
+            )
 
         def spread_q(unit):
-            n, quarter = divmod(unit, QUARTERS)
-            t0 = quarter * GROUPS_PER_UNIT
+            n, part = divmod(unit, PARTS)
+            t0 = part * GROUPS_PER_UNIT
             q_of_groups = qk_turned_of[n][:, t0 : t0 + GROUPS_PER_UNIT, 0:HEADS]
             q_blocks = block_pool.tile([P, GROUPS_PER_UNIT, SLOTS, HEADS], F32)
             for j in range(SLOTS):
@@ -219,28 +213,29 @@ def tile_attention_pa_t_kernel(tc, x, w_qk, b_qk, out):
                     )
             q_blocks_of[unit] = q_blocks
 
-        def scores(unit):
-            n, quarter = divmod(unit, QUARTERS)
-            t0 = quarter * GROUPS_PER_UNIT
-            score = psum_score.tile([P, GROUPS_PER_UNIT, HEADS], F32)
-            for i in range(GROUPS_PER_UNIT):
+        def scores(unit, half):
+            n, part = divmod(unit, PARTS)
+            t0 = part * GROUPS_PER_UNIT
+            if half == 0:
+                score = psum_score.tile([P, GROUPS_PER_UNIT, SCORE_COLS], F32)
+                score_of[unit] = score
+            for i in range(half * GROUPS_PER_UNIT // 2, (half + 1) * GROUPS_PER_UNIT // 2):
                 nc.tensor.matmul(
-                    out=score[:, i, :],
+                    out=score_of[unit][:, i, :],
                     lhsT=q_blocks_of[unit][:, i, :, :].rearrange("p j h -> p (j h)"),
-                    rhs=qk_turned_of[n][:, t0 + i, HEADS:QK_HEADS],
+                    rhs=qk_turned_of[n][:, t0 + i, HEADS - RIDE_ALONG : QK_HEADS],
                     start=True,
                     stop=True,
                 )
-            score_of[unit] = score
 
         def subtract_top(unit):
-            score = score_of[unit]
+            score = score_of[unit][:, :, RIDE_ALONG:SCORE_COLS]
             top = soft_pool.tile([P, GROUPS_PER_UNIT], F32)
-            nc.vector.tensor_reduce(out=top[:], in_=score[:], axis=AXIS.X, op=ALU.max)
+            nc.vector.tensor_reduce(out=top[:], in_=score, axis=AXIS.X, op=ALU.max)
             prob = soft_pool.tile([P, GROUPS_PER_UNIT, HEADS], F32)
             nc.vector.tensor_tensor(
                 out=prob[:],
-                in0=score[:],
+                in0=score,
                 in1=top[:].unsqueeze(2).to_broadcast([P, GROUPS_PER_UNIT, HEADS]),
                 op=ALU.subtract,
             )
@@ -250,7 +245,7 @@ def tile_attention_pa_t_kernel(tc, x, w_qk, b_qk, out):
             nc.scalar.activation(out=prob_of[unit][:], in_=prob_of[unit][:], func=ACT.Exp)
 
         def normalise_and_store(unit):
-            n, quarter = divmod(unit, QUARTERS)
+            n, part = divmod(unit, PARTS)
             prob = prob_of[unit]
             total = soft_pool.tile([P, GROUPS_PER_UNIT], F32)
             nc.vector.tensor_reduce(out=total[:], in_=prob[:], axis=AXIS.X, op=ALU.add)
@@ -262,7 +257,7 @@ def tile_attention_pa_t_kernel(tc, x, w_qk, b_qk, out):
                 in1=inverse[:].unsqueeze(2).to_broadcast([P, GROUPS_PER_UNIT, HEADS]),
                 op=ALU.mult,
             )
-            first = quarter * GROUPS_PER_UNIT * SLOTS
+            first = part * GROUPS_PER_UNIT * SLOTS
             nc.sync.dma_start(
                 out=out[n, first : first + GROUPS_PER_UNIT * SLOTS].rearrange(
                     "(t j) h g -> (j h) t g", j=SLOTS
@@ -270,19 +265,22 @@ def tile_attention_pa_t_kernel(tc, x, w_qk, b_qk, out):
                 in_=prob[:],
             )
 
-        def run(stage, unit):
+        def run(stage, unit, *part_of_stage):
             if 0 <= unit < UNITS:
-                stage(unit)
+                stage(unit, *part_of_stage)
 
         for step in range(UNITS + SOFTMAX_LAG):
             run(load_x, step + LOAD_AHEAD)
             run(keep_turned, step - KEEP_LAG)
             run(subtract_top, step - SOFTMAX_LAG)
-            run(project, step - PROJECT_LAG)
             run(exponential, step - SOFTMAX_LAG)
-            run(turn_x, step)
             run(spread_q, step - SPREAD_LAG)
+            run(project_pass, step - PROJECT_LAG, 0)
+            run(scores, step - SCORE_LAG, 0)
+            run(turn_x, step)
+            run(project_pass, step - PROJECT_LAG, 1)
+            run(add_bias, step - PROJECT_LAG)
             run(quantise_x, step)
-            run(scores, step - SCORE_LAG)
             run(normalise_and_store, step - SOFTMAX_LAG)
+            run(scores, step - SCORE_LAG, 1)
             run(turn_qk, step - TURN_LAG)

@@ -18,29 +18,21 @@ TOKENS = 1024
 K = 1024
 HEADS = 16
 HD = 16
-QK_HEADS = 2 * HEADS
-QK_COLS = QK_HEADS * HD
+Q_COLS = HEADS * HD
+QK_COLS = 2 * Q_COLS
 PACK = 4
 PASSES = K // (P * PACK)
 WORD_TILES = K // 2 // P
-SLOTS = TOKENS // P
-
-PARTS = SLOTS
-UNITS = BATCH * PARTS
-HEADS_PER_BANK = QK_HEADS // PARTS
-GROUPS_PER_UNIT = P // PARTS
-RIDE_ALONG = 8
-SCORE_COLS = RIDE_ALONG + HEADS
+TILES = TOKENS // P
+UNITS = BATCH * TILES
+PAIR_BLOCKS = HEADS * HEADS // P
+HEADS_PER_BLOCK = HEADS // PAIR_BLOCKS
 
 LOAD_AHEAD = 4
 PROJECT_LAG = 1
-TURN_LAG = PARTS - 1 + PROJECT_LAG
-KEEP_LAG = TURN_LAG + 1
-SCORE_LAG = KEEP_LAG + PARTS - 1
-SPREAD_LAG = SCORE_LAG - 1
-SOFTMAX_LAG = SCORE_LAG + 1
-
-SPREAD_ON_SCALAR = 3
+SUM_LAG = PROJECT_LAG + 1
+BACK_LAG = SUM_LAG + 1
+SOFTMAX_LAG = BACK_LAG + 1
 
 FLOPS = 2 * BATCH * TOKENS * K * QK_COLS + 2 * BATCH * TOKENS * HEADS * HEADS * HD
 
@@ -51,47 +43,33 @@ def tile_attention_pa_t_kernel(tc, x, w_qk, b_qk, out):
         stack.enter_context(tc.manual_schedule())
         const = stack.enter_context(tc.tile_pool(name="const", bufs=1))
         x_pool = stack.enter_context(tc.tile_pool(name="x_pool", bufs=LOAD_AHEAD + 1))
-        mx_pool = stack.enter_context(tc.tile_pool(name="mx_pool", bufs=2))
-        batch_pool = stack.enter_context(tc.tile_pool(name="batch_pool", bufs=2))
-        block_pool = stack.enter_context(tc.tile_pool(name="block_pool", bufs=2))
+        work = stack.enter_context(tc.tile_pool(name="work", bufs=2))
         soft_pool = stack.enter_context(tc.tile_pool(name="soft_pool", bufs=3))
         psum_xt = stack.enter_context(tc.psum_pool(name="psum_xt", bufs=2))
         psum_qk = stack.enter_context(tc.psum_pool(name="psum_qk", bufs=2))
-        psum_turn = stack.enter_context(tc.psum_pool(name="psum_turn", bufs=2))
-        psum_score = stack.enter_context(tc.psum_pool(name="psum_score", bufs=2))
+        psum_sum = stack.enter_context(tc.psum_pool(name="psum_sum", bufs=2))
+        psum_back = stack.enter_context(tc.psum_pool(name="psum_back", bufs=2))
 
         x_rows_of = {}
         x_grouped_of = {}
         x_mx_of = {}
         qk_sum_of = {}
-        qk_rows_of = {}
-        turned_of = {}
-        qk_turned_of = {}
-        q_blocks_of = {}
+        products_of = {}
+        pair_rows_of = {}
+        pair_rows_kept_of = {}
         score_of = {}
         prob_of = {}
 
         def load_x(unit):
-            n, j = divmod(unit, PARTS)
+            n, j = divmod(unit, TILES)
             x_rows = x_pool.tile([P, K], BF16)
-            nc.sync.dma_start(out=x_rows[:], in_=x[n].rearrange("(t j) k -> t j k", j=SLOTS)[:, j, :])
+            nc.sync.dma_start(out=x_rows[:], in_=x[n].rearrange("(t j) k -> t j k", j=TILES)[:, j, :])
             x_rows_of[unit] = x_rows
 
         load_x(0)
 
         ident = const.tile([P, P], F32)
         make_identity(nc, ident[:])
-        slot_of_partition = const.tile([P, SLOTS], F32)
-        nc.vector.tensor_reduce(
-            out=slot_of_partition[:],
-            in_=ident[:].rearrange("p (j d) -> p j d", d=HD),
-            axis=AXIS.X,
-            op=ALU.add,
-        )
-        slot_mask = const.tile([P, SLOTS], F32)
-        nc.vector.tensor_scalar(
-            out=slot_mask[:], in0=slot_of_partition[:], scalar1=HD**-0.5, scalar2=None, op0=ALU.mult
-        )
 
         w_codes = const.tile([P, PASSES, QK_COLS], U32, align_bytes=64)
         w_scales = const.tile([P, PASSES, QK_COLS], U8, align_bytes=64)
@@ -104,7 +82,12 @@ def tile_attention_pa_t_kernel(tc, x, w_qk, b_qk, out):
                     in_=w_qk[first : first + 2 * P, :].rearrange("(p e) n -> p e n", e=2),
                 )
             w_grouped = const.tile([P, QK_COLS, PACK], BF16, align_bytes=64, name="w_grouped%d" % c)
-            nc.vector.tensor_copy(out=w_grouped[:], in_=w_rows[:].rearrange("p v n -> p n v"))
+            for half in range(2):
+                cols = slice(half * Q_COLS, (half + 1) * Q_COLS)
+                nc.vector.tensor_copy(
+                    out=w_grouped[:, cols, :].rearrange("p (d h) v -> p d h v", d=HD),
+                    in_=w_rows[:, :, cols].rearrange("p v (h d) -> p d h v", d=HD),
+                )
             nc.vector.quantize_mx(
                 out=w_codes[:, c, :].bitcast(FP8X4),
                 scales=w_scales[:, c, :],
@@ -114,7 +97,10 @@ def tile_attention_pa_t_kernel(tc, x, w_qk, b_qk, out):
         bias_bf16 = const.tile([P, QK_COLS], BF16)
         nc.sync.dma_start(out=bias_bf16[:], in_=b_qk.partition_broadcast(P))
         bias = const.tile([P, QK_COLS], F32)
-        nc.vector.tensor_copy(out=bias[:], in_=bias_bf16[:])
+        nc.vector.tensor_copy(
+            out=bias[:].rearrange("p (c d h) -> p c d h", c=2, d=HD),
+            in_=bias_bf16[:].rearrange("p (c h d) -> p c d h", c=2, d=HD),
+        )
 
         for unit in range(1, LOAD_AHEAD):
             load_x(unit)
@@ -124,7 +110,7 @@ def tile_attention_pa_t_kernel(tc, x, w_qk, b_qk, out):
             x_turned = psum_xt.tile([P, WORD_TILES, P], F32)
             for w in range(WORD_TILES):
                 nc.tensor.transpose(x_turned[:, w, :], x_words[:, w * P : (w + 1) * P], ident[:])
-            x_grouped = mx_pool.tile([P, K], BF16, align_bytes=64)
+            x_grouped = work.tile([P, K], BF16, align_bytes=64)
             nc.scalar.copy(
                 out=x_grouped[:].bitcast(F32).rearrange("p (c t u) -> p c t u", c=PASSES, u=2),
                 in_=x_turned[:].rearrange("p (c u) t -> p c t u", u=2),
@@ -132,8 +118,8 @@ def tile_attention_pa_t_kernel(tc, x, w_qk, b_qk, out):
             x_grouped_of[unit] = x_grouped
 
         def quantise_x(unit):
-            x_codes = mx_pool.tile([P, PASSES, P], U32, align_bytes=64)
-            x_scales = mx_pool.tile([P, PASSES, P], U8, align_bytes=64)
+            x_codes = work.tile([P, PASSES, P], U32, align_bytes=64)
+            x_scales = work.tile([P, PASSES, P], U8, align_bytes=64)
             nc.vector.quantize_mx(
                 out=x_codes[:].rearrange("p c t -> p (c t)").bitcast(FP8X4),
                 scales=x_scales[:].rearrange("p c t -> p (c t)"),
@@ -141,146 +127,121 @@ def tile_attention_pa_t_kernel(tc, x, w_qk, b_qk, out):
             )
             x_mx_of[unit] = (x_codes, x_scales)
 
-        def project_pass(unit, c):
-            if c == 0:
-                qk_sum = psum_qk.tile([P, QK_COLS], F32)
-                qk_sum_of[unit] = qk_sum
+        def project(unit):
             x_codes, x_scales = x_mx_of[unit]
-            nc.tensor.matmul_mx(
-                out=qk_sum_of[unit][:],
-                lhsT=x_codes[:, c, :].bitcast(FP8X4),
-                lhsT_scale=x_scales[:, c, :],
-                rhs=w_codes[:, c, :].bitcast(FP8X4),
-                rhs_scale=w_scales[:, c, :],
-                start=(c == 0),
-                stop=(c == PASSES - 1),
-            )
+            qk_sum = psum_qk.tile([P, QK_COLS], F32)
+            for c in range(PASSES):
+                nc.tensor.matmul_mx(
+                    out=qk_sum[:],
+                    lhsT=x_codes[:, c, :].bitcast(FP8X4),
+                    lhsT_scale=x_scales[:, c, :],
+                    rhs=w_codes[:, c, :].bitcast(FP8X4),
+                    rhs_scale=w_scales[:, c, :],
+                    start=(c == 0),
+                    stop=(c == PASSES - 1),
+                )
+            qk_sum_of[unit] = qk_sum
 
-        def add_bias(unit):
-            n, j = divmod(unit, PARTS)
-            if j == 0:
-                qk_rows = batch_pool.tile([P, QK_HEADS, SLOTS, HD], F32)
-                qk_rows_of[n] = qk_rows
+        def multiply_heads(unit):
+            qk = work.tile([P, QK_COLS], F32)
+            nc.vector.tensor_tensor(out=qk[:], in0=qk_sum_of[unit][:], in1=bias[:], op=ALU.add)
+            products = work.tile([P, HD, HEADS, HEADS], F32)
             nc.vector.tensor_tensor(
-                out=qk_rows_of[n][:, :, j, :],
-                in0=qk_sum_of[unit][:].rearrange("p (h d) -> p h d", d=HD),
-                in1=bias[:].rearrange("p (h d) -> p h d", d=HD),
-                op=ALU.add,
+                out=products[:],
+                in0=qk[:, 0:Q_COLS]
+                .rearrange("p (d h) -> p d h", d=HD)
+                .unsqueeze(3)
+                .to_broadcast([P, HD, HEADS, HEADS]),
+                in1=qk[:, Q_COLS:QK_COLS]
+                .rearrange("p (d g) -> p d g", d=HD)
+                .unsqueeze(2)
+                .to_broadcast([P, HD, HEADS, HEADS]),
+                op=ALU.mult,
             )
+            products_of[unit] = products
 
-        def turn_qk(unit):
-            n, part = divmod(unit, PARTS)
-            turned = psum_turn.tile([P, HEADS_PER_BANK, P], F32)
-            for h in range(HEADS_PER_BANK):
+        def sum_over_d(unit):
+            pair_rows = psum_sum.tile([P, PAIR_BLOCKS, P], F32)
+            for b in range(PAIR_BLOCKS):
+                h0 = b * HEADS_PER_BLOCK
+                for d in range(HD):
+                    nc.tensor.matmul(
+                        out=pair_rows[:, b, :],
+                        lhsT=products_of[unit][:, d, h0 : h0 + HEADS_PER_BLOCK, :].rearrange(
+                            "p h g -> p (h g)"
+                        ),
+                        rhs=ident[:],
+                        is_transpose=True,
+                        start=(d == 0),
+                        stop=(d == HD - 1),
+                    )
+            pair_rows_of[unit] = pair_rows
+
+        def keep_pair_rows(unit):
+            pair_rows_kept = work.tile([P, PAIR_BLOCKS, P], F32)
+            nc.scalar.copy(out=pair_rows_kept[:], in_=pair_rows_of[unit][:])
+            pair_rows_kept_of[unit] = pair_rows_kept
+
+        def turn_back(unit):
+            score = psum_back.tile([P, HEADS, HEADS], F32)
+            for b in range(PAIR_BLOCKS):
+                h0 = b * HEADS_PER_BLOCK
                 nc.tensor.transpose(
-                    turned[:, h, :],
-                    qk_rows_of[n][:, part * HEADS_PER_BANK + h, :, :].rearrange("p j d -> p (j d)"),
+                    score[:, h0 : h0 + HEADS_PER_BLOCK, :].rearrange("p h g -> p (h g)"),
+                    pair_rows_kept_of[unit][:, b, :],
                     ident[:],
                 )
-            turned_of[unit] = turned
-
-        def keep_turned(unit):
-            n, part = divmod(unit, PARTS)
-            if part == 0:
-                qk_turned = batch_pool.tile([P, P, QK_HEADS], F32)
-                qk_turned_of[n] = qk_turned
-            head0 = part * HEADS_PER_BANK
-            nc.scalar.copy(
-                out=qk_turned_of[n][:, :, head0 : head0 + HEADS_PER_BANK],
-                in_=turned_of[unit][:].rearrange("p h t -> p t h"),
-            )
-
-        def spread_q(unit):
-            n, part = divmod(unit, PARTS)
-            t0 = part * GROUPS_PER_UNIT
-            q_of_groups = qk_turned_of[n][:, t0 : t0 + GROUPS_PER_UNIT, 0:HEADS]
-            q_blocks = block_pool.tile([P, GROUPS_PER_UNIT, SLOTS, HEADS], F32)
-            for j in range(SLOTS):
-                if j < SPREAD_ON_SCALAR:
-                    nc.scalar.activation(
-                        out=q_blocks[:, :, j, :],
-                        in_=q_of_groups,
-                        func=ACT.Copy,
-                        scale=slot_mask[:, j : j + 1],
-                    )
-                else:
-                    nc.vector.tensor_scalar(
-                        out=q_blocks[:, :, j, :],
-                        in0=q_of_groups,
-                        scalar1=slot_mask[:, j : j + 1],
-                        scalar2=None,
-                        op0=ALU.mult,
-                    )
-            q_blocks_of[unit] = q_blocks
-
-        def scores(unit, half):
-            n, part = divmod(unit, PARTS)
-            t0 = part * GROUPS_PER_UNIT
-            if half == 0:
-                score = psum_score.tile([P, GROUPS_PER_UNIT, SCORE_COLS], F32)
-                score_of[unit] = score
-            for i in range(half * GROUPS_PER_UNIT // 2, (half + 1) * GROUPS_PER_UNIT // 2):
-                nc.tensor.matmul(
-                    out=score_of[unit][:, i, :],
-                    lhsT=q_blocks_of[unit][:, i, :, :].rearrange("p j h -> p (j h)"),
-                    rhs=qk_turned_of[n][:, t0 + i, HEADS - RIDE_ALONG : QK_HEADS],
-                    start=True,
-                    stop=True,
-                )
+            score_of[unit] = score
 
         def subtract_top(unit):
-            score = score_of[unit][:, :, RIDE_ALONG:SCORE_COLS]
-            top = soft_pool.tile([P, GROUPS_PER_UNIT], F32)
-            nc.vector.tensor_reduce(out=top[:], in_=score, axis=AXIS.X, op=ALU.max)
-            prob = soft_pool.tile([P, GROUPS_PER_UNIT, HEADS], F32)
+            score = score_of[unit]
+            top = soft_pool.tile([P, HEADS], F32)
+            nc.vector.tensor_reduce(out=top[:], in_=score[:], axis=AXIS.X, op=ALU.max)
+            prob = soft_pool.tile([P, HEADS, HEADS], F32)
             nc.vector.tensor_tensor(
                 out=prob[:],
-                in0=score,
-                in1=top[:].unsqueeze(2).to_broadcast([P, GROUPS_PER_UNIT, HEADS]),
+                in0=score[:],
+                in1=top[:].unsqueeze(2).to_broadcast([P, HEADS, HEADS]),
                 op=ALU.subtract,
             )
             prob_of[unit] = prob
 
         def exponential(unit):
-            nc.scalar.activation(out=prob_of[unit][:], in_=prob_of[unit][:], func=ACT.Exp)
+            nc.scalar.activation(
+                out=prob_of[unit][:], in_=prob_of[unit][:], func=ACT.Exp, scale=HD**-0.5
+            )
 
         def normalise_and_store(unit):
-            n, part = divmod(unit, PARTS)
+            n, j = divmod(unit, TILES)
             prob = prob_of[unit]
-            total = soft_pool.tile([P, GROUPS_PER_UNIT], F32)
+            total = soft_pool.tile([P, HEADS], F32)
             nc.vector.tensor_reduce(out=total[:], in_=prob[:], axis=AXIS.X, op=ALU.add)
-            inverse = soft_pool.tile([P, GROUPS_PER_UNIT], F32)
+            inverse = soft_pool.tile([P, HEADS], F32)
             nc.vector.reciprocal(out=inverse[:], in_=total[:])
             nc.vector.tensor_tensor(
                 out=prob[:],
                 in0=prob[:],
-                in1=inverse[:].unsqueeze(2).to_broadcast([P, GROUPS_PER_UNIT, HEADS]),
+                in1=inverse[:].unsqueeze(2).to_broadcast([P, HEADS, HEADS]),
                 op=ALU.mult,
             )
-            first = part * GROUPS_PER_UNIT * SLOTS
             nc.sync.dma_start(
-                out=out[n, first : first + GROUPS_PER_UNIT * SLOTS].rearrange(
-                    "(t j) h g -> (j h) t g", j=SLOTS
-                ),
-                in_=prob[:],
+                out=out[n].rearrange("(t j) h g -> t j (h g)", j=TILES)[:, j, :],
+                in_=prob[:].rearrange("p h g -> p (h g)"),
             )
 
-        def run(stage, unit, *part_of_stage):
+        def run(stage, unit):
             if 0 <= unit < UNITS:
-                stage(unit, *part_of_stage)
+                stage(unit)
 
         for step in range(UNITS + SOFTMAX_LAG):
             run(load_x, step + LOAD_AHEAD)
-            run(keep_turned, step - KEEP_LAG)
+            run(keep_pair_rows, step - BACK_LAG)
             run(subtract_top, step - SOFTMAX_LAG)
             run(exponential, step - SOFTMAX_LAG)
-            run(spread_q, step - SPREAD_LAG)
-            run(project_pass, step - PROJECT_LAG, 0)
-            run(scores, step - SCORE_LAG, 0)
+            run(project, step - PROJECT_LAG)
+            run(multiply_heads, step - PROJECT_LAG)
             run(turn_x, step)
-            run(project_pass, step - PROJECT_LAG, 1)
-            run(add_bias, step - PROJECT_LAG)
             run(quantise_x, step)
             run(normalise_and_store, step - SOFTMAX_LAG)
-            run(scores, step - SCORE_LAG, 1)
-            run(turn_qk, step - TURN_LAG)
+            run(sum_over_d, step - SUM_LAG)
+            run(turn_back, step - BACK_LAG)

@@ -30,9 +30,11 @@ HEADS_PER_BLOCK = HEADS // PAIR_BLOCKS
 
 LOAD_AHEAD = 4
 PROJECT_LAG = 1
-SUM_LAG = PROJECT_LAG + 1
+MULTIPLY_LAG = PROJECT_LAG + 1
+SUM_LAG = MULTIPLY_LAG + 1
 BACK_LAG = SUM_LAG + 1
-SOFTMAX_LAG = BACK_LAG + 1
+SHIFT_LAG = BACK_LAG + 1
+NORMALISE_LAG = SHIFT_LAG + 1
 
 FLOPS = 2 * BATCH * TOKENS * K * QK_COLS + 2 * BATCH * TOKENS * HEADS * HEADS * HD
 
@@ -54,11 +56,15 @@ def tile_attention_pa_t_kernel(tc, x, w_qk, b_qk, out):
         x_grouped_of = {}
         x_mx_of = {}
         qk_sum_of = {}
+        qk_of = {}
         products_of = {}
         pair_rows_of = {}
         pair_rows_kept_of = {}
         score_of = {}
+        top_of = {}
         prob_of = {}
+        total_of = {}
+        inverse_of = {}
 
         def load_x(unit):
             n, j = divmod(unit, TILES)
@@ -142,9 +148,13 @@ def tile_attention_pa_t_kernel(tc, x, w_qk, b_qk, out):
                 )
             qk_sum_of[unit] = qk_sum
 
-        def multiply_heads(unit):
+        def add_bias(unit):
             qk = work.tile([P, QK_COLS], F32)
             nc.vector.tensor_tensor(out=qk[:], in0=qk_sum_of[unit][:], in1=bias[:], op=ALU.add)
+            qk_of[unit] = qk
+
+        def multiply_heads(unit):
+            qk = qk_of[unit]
             products = work.tile([P, HD, HEADS, HEADS], F32)
             nc.vector.tensor_tensor(
                 out=products[:],
@@ -193,10 +203,14 @@ def tile_attention_pa_t_kernel(tc, x, w_qk, b_qk, out):
                 )
             score_of[unit] = score
 
+        def find_top(unit):
+            top = soft_pool.tile([P, HEADS], F32)
+            nc.vector.tensor_reduce(out=top[:], in_=score_of[unit][:], axis=AXIS.X, op=ALU.max)
+            top_of[unit] = top
+
         def subtract_top(unit):
             score = score_of[unit]
-            top = soft_pool.tile([P, HEADS], F32)
-            nc.vector.tensor_reduce(out=top[:], in_=score[:], axis=AXIS.X, op=ALU.max)
+            top = top_of[unit]
             prob = soft_pool.tile([P, HEADS, HEADS], F32)
             nc.vector.tensor_tensor(
                 out=prob[:],
@@ -211,13 +225,20 @@ def tile_attention_pa_t_kernel(tc, x, w_qk, b_qk, out):
                 out=prob_of[unit][:], in_=prob_of[unit][:], func=ACT.Exp, scale=HD**-0.5
             )
 
-        def normalise_and_store(unit):
+        def add_up(unit):
+            total = soft_pool.tile([P, HEADS], F32)
+            nc.vector.tensor_reduce(out=total[:], in_=prob_of[unit][:], axis=AXIS.X, op=ALU.add)
+            total_of[unit] = total
+
+        def invert(unit):
+            inverse = soft_pool.tile([P, HEADS], F32)
+            nc.vector.reciprocal(out=inverse[:], in_=total_of[unit][:])
+            inverse_of[unit] = inverse
+
+        def scale_and_store(unit):
             n, j = divmod(unit, TILES)
             prob = prob_of[unit]
-            total = soft_pool.tile([P, HEADS], F32)
-            nc.vector.tensor_reduce(out=total[:], in_=prob[:], axis=AXIS.X, op=ALU.add)
-            inverse = soft_pool.tile([P, HEADS], F32)
-            nc.vector.reciprocal(out=inverse[:], in_=total[:])
+            inverse = inverse_of[unit]
             nc.vector.tensor_tensor(
                 out=prob[:],
                 in0=prob[:],
@@ -233,15 +254,19 @@ def tile_attention_pa_t_kernel(tc, x, w_qk, b_qk, out):
             if 0 <= unit < UNITS:
                 stage(unit)
 
-        for step in range(UNITS + SOFTMAX_LAG):
+        for step in range(UNITS + NORMALISE_LAG):
             run(load_x, step + LOAD_AHEAD)
             run(keep_pair_rows, step - BACK_LAG)
-            run(subtract_top, step - SOFTMAX_LAG)
-            run(exponential, step - SOFTMAX_LAG)
             run(project, step - PROJECT_LAG)
-            run(multiply_heads, step - PROJECT_LAG)
+            run(add_bias, step - MULTIPLY_LAG)
+            run(find_top, step - SHIFT_LAG)
+            run(add_up, step - NORMALISE_LAG)
+            run(multiply_heads, step - MULTIPLY_LAG)
             run(turn_x, step)
+            run(subtract_top, step - SHIFT_LAG)
+            run(exponential, step - SHIFT_LAG)
+            run(invert, step - NORMALISE_LAG)
             run(quantise_x, step)
-            run(normalise_and_store, step - SOFTMAX_LAG)
+            run(scale_and_store, step - NORMALISE_LAG)
             run(sum_over_d, step - SUM_LAG)
             run(turn_back, step - BACK_LAG)

@@ -62,6 +62,7 @@ def tile_attention_pa_t_kernel(tc, x, w_qk, b_qk, out):
         pair_rows_kept_of = {}
         score_of = {}
         top_of = {}
+        shift_of = {}
         prob_of = {}
         total_of = {}
         inverse_of = {}
@@ -208,26 +209,26 @@ def tile_attention_pa_t_kernel(tc, x, w_qk, b_qk, out):
             nc.vector.tensor_reduce(out=top[:], in_=score_of[unit][:], axis=AXIS.X, op=ALU.max)
             top_of[unit] = top
 
-        def subtract_top(unit):
-            score = score_of[unit]
-            top = top_of[unit]
-            prob = soft_pool.tile([P, HEADS, HEADS], F32)
-            nc.vector.tensor_tensor(
-                out=prob[:],
-                in0=score[:],
-                in1=top[:].unsqueeze(2).to_broadcast([P, HEADS, HEADS]),
-                op=ALU.subtract,
+        def negate_top(unit):
+            shift = soft_pool.tile([P, HEADS], F32)
+            nc.vector.tensor_scalar(
+                out=shift[:], in0=top_of[unit][:], scalar1=-(HD**-0.5), scalar2=None, op0=ALU.mult
             )
-            prob_of[unit] = prob
+            shift_of[unit] = shift
 
         def exponential(unit):
-            nc.scalar.activation(
-                out=prob_of[unit][:], in_=prob_of[unit][:], func=ACT.Exp, scale=HD**-0.5
-            )
-
-        def add_up(unit):
+            prob = soft_pool.tile([P, HEADS, HEADS], F32)
             total = soft_pool.tile([P, HEADS], F32)
-            nc.vector.tensor_reduce(out=total[:], in_=prob_of[unit][:], axis=AXIS.X, op=ALU.add)
+            for h in range(HEADS):
+                nc.scalar.activation(
+                    out=prob[:, h, :],
+                    in_=score_of[unit][:, h, :],
+                    func=ACT.Exp,
+                    bias=shift_of[unit][:, h : h + 1],
+                    scale=HD**-0.5,
+                    accum_out=total[:, h : h + 1],
+                )
+            prob_of[unit] = prob
             total_of[unit] = total
 
         def invert(unit):
@@ -258,14 +259,13 @@ def tile_attention_pa_t_kernel(tc, x, w_qk, b_qk, out):
             run(load_x, step + LOAD_AHEAD)
             run(keep_pair_rows, step - BACK_LAG)
             run(project, step - PROJECT_LAG)
-            run(add_bias, step - MULTIPLY_LAG)
             run(find_top, step - SHIFT_LAG)
-            run(add_up, step - NORMALISE_LAG)
-            run(multiply_heads, step - MULTIPLY_LAG)
-            run(turn_x, step)
-            run(subtract_top, step - SHIFT_LAG)
+            run(add_bias, step - MULTIPLY_LAG)
+            run(negate_top, step - SHIFT_LAG)
             run(exponential, step - SHIFT_LAG)
             run(invert, step - NORMALISE_LAG)
+            run(multiply_heads, step - MULTIPLY_LAG)
+            run(turn_x, step)
             run(quantise_x, step)
             run(scale_and_store, step - NORMALISE_LAG)
             run(sum_over_d, step - SUM_LAG)

@@ -239,13 +239,13 @@ def tile_attention_pa_t_kernel(tc, x, w_qk, b_qk, out):
         def scale_and_store(unit):
             n, j = divmod(unit, TILES)
             prob = prob_of[unit]
-            inverse = inverse_of[unit]
-            nc.vector.tensor_tensor(
-                out=prob[:],
-                in0=prob[:],
-                in1=inverse[:].unsqueeze(2).to_broadcast([P, HEADS, HEADS]),
-                op=ALU.mult,
-            )
+            for h in range(HEADS):
+                nc.scalar.activation(
+                    out=prob[:, h, :],
+                    in_=prob[:, h, :],
+                    func=ACT.Copy,
+                    scale=inverse_of[unit][:, h : h + 1],
+                )
             nc.sync.dma_start(
                 out=out[n].rearrange("(t j) h g -> t j (h g)", j=TILES)[:, j, :],
                 in_=prob[:].rearrange("p h g -> p (h g)"),

@@ -27,9 +27,12 @@ TILES = TOKENS // P
 UNITS = BATCH * TILES
 PAIR_BLOCKS = HEADS * HEADS // P
 HEADS_PER_BLOCK = HEADS // PAIR_BLOCKS
+D_ON_GPSIMD = 2
+D_ON_VECTOR = HD - D_ON_GPSIMD
 
 LOAD_AHEAD = 4
-PROJECT_LAG = 1
+QUANTISE_LAG = 1
+PROJECT_LAG = QUANTISE_LAG + 1
 MULTIPLY_LAG = PROJECT_LAG + 1
 SUM_LAG = MULTIPLY_LAG + 1
 BACK_LAG = SUM_LAG + 1
@@ -47,6 +50,7 @@ def tile_attention_pa_t_kernel(tc, x, w_qk, b_qk, out):
         x_pool = stack.enter_context(tc.tile_pool(name="x_pool", bufs=LOAD_AHEAD + 1))
         work = stack.enter_context(tc.tile_pool(name="work", bufs=2))
         soft_pool = stack.enter_context(tc.tile_pool(name="soft_pool", bufs=3))
+        gpsimd_pool = stack.enter_context(tc.tile_pool(name="gpsimd_pool", bufs=1))
         psum_xt = stack.enter_context(tc.psum_pool(name="psum_xt", bufs=2))
         psum_qk = stack.enter_context(tc.psum_pool(name="psum_qk", bufs=2))
         psum_sum = stack.enter_context(tc.psum_pool(name="psum_sum", bufs=2))
@@ -58,6 +62,7 @@ def tile_attention_pa_t_kernel(tc, x, w_qk, b_qk, out):
         qk_sum_of = {}
         qk_of = {}
         products_of = {}
+        last_products_of = {}
         pair_rows_of = {}
         pair_rows_kept_of = {}
         score_of = {}
@@ -154,33 +159,43 @@ def tile_attention_pa_t_kernel(tc, x, w_qk, b_qk, out):
             nc.vector.tensor_tensor(out=qk[:], in0=qk_sum_of[unit][:], in1=bias[:], op=ALU.add)
             qk_of[unit] = qk
 
-        def multiply_heads(unit):
-            qk = qk_of[unit]
-            products = work.tile([P, HD, HEADS, HEADS], F32)
-            nc.vector.tensor_tensor(
+        def multiply(engine, products, qk, d0, d1):
+            shape = [P, d1 - d0, HEADS, HEADS]
+            engine.tensor_tensor(
                 out=products[:],
                 in0=qk[:, 0:Q_COLS]
-                .rearrange("p (d h) -> p d h", d=HD)
+                .rearrange("p (d h) -> p d h", d=HD)[:, d0:d1, :]
                 .unsqueeze(3)
-                .to_broadcast([P, HD, HEADS, HEADS]),
+                .to_broadcast(shape),
                 in1=qk[:, Q_COLS:QK_COLS]
-                .rearrange("p (d g) -> p d g", d=HD)
+                .rearrange("p (d g) -> p d g", d=HD)[:, d0:d1, :]
                 .unsqueeze(2)
-                .to_broadcast([P, HD, HEADS, HEADS]),
+                .to_broadcast(shape),
                 op=ALU.mult,
             )
+
+        def multiply_heads(unit):
+            products = work.tile([P, D_ON_VECTOR, HEADS, HEADS], F32)
+            multiply(nc.vector, products, qk_of[unit], 0, D_ON_VECTOR)
             products_of[unit] = products
+
+        def multiply_last_d(unit):
+            last_products = gpsimd_pool.tile([P, D_ON_GPSIMD, HEADS, HEADS], F32)
+            multiply(nc.gpsimd, last_products, qk_of[unit], D_ON_VECTOR, HD)
+            last_products_of[unit] = last_products
 
         def sum_over_d(unit):
             pair_rows = psum_sum.tile([P, PAIR_BLOCKS, P], F32)
             for b in range(PAIR_BLOCKS):
                 h0 = b * HEADS_PER_BLOCK
                 for d in range(HD):
+                    if d < D_ON_VECTOR:
+                        of_d = products_of[unit][:, d, :, :]
+                    else:
+                        of_d = last_products_of[unit][:, d - D_ON_VECTOR, :, :]
                     nc.tensor.matmul(
                         out=pair_rows[:, b, :],
-                        lhsT=products_of[unit][:, d, h0 : h0 + HEADS_PER_BLOCK, :].rearrange(
-                            "p h g -> p (h g)"
-                        ),
+                        lhsT=of_d[:, h0 : h0 + HEADS_PER_BLOCK, :].rearrange("p h g -> p (h g)"),
                         rhs=ident[:],
                         is_transpose=True,
                         start=(d == 0),
@@ -257,6 +272,7 @@ def tile_attention_pa_t_kernel(tc, x, w_qk, b_qk, out):
 
         for step in range(UNITS + NORMALISE_LAG):
             run(load_x, step + LOAD_AHEAD)
+            run(multiply_last_d, step - SUM_LAG)
             run(keep_pair_rows, step - BACK_LAG)
             run(project, step - PROJECT_LAG)
             run(find_top, step - SHIFT_LAG)
@@ -264,9 +280,9 @@ def tile_attention_pa_t_kernel(tc, x, w_qk, b_qk, out):
             run(negate_top, step - SHIFT_LAG)
             run(exponential, step - SHIFT_LAG)
             run(invert, step - NORMALISE_LAG)
+            run(quantise_x, step - QUANTISE_LAG)
             run(multiply_heads, step - MULTIPLY_LAG)
             run(turn_x, step)
-            run(quantise_x, step)
             run(scale_and_store, step - NORMALISE_LAG)
             run(sum_over_d, step - SUM_LAG)
             run(turn_back, step - BACK_LAG)

from contextlib import ExitStack

import concourse.mybir as mybir
from concourse.masks import make_identity

F32 = mybir.dt.float32
BF16 = mybir.dt.bfloat16
U32 = mybir.dt.uint32
U8 = mybir.dt.uint8
FP8X4 = mybir.dt.float8_e4m3fn_x4
ALU = mybir.AluOpType
ACT = mybir.ActivationFunctionType
AXIS = mybir.AxisListType

P = 128
BATCH = 8
TOKENS = 1024
K = 1024
HEADS = 16
HD = 16
Q_COLS = HEADS * HD
QK_COLS = 2 * Q_COLS
PACK = 4
PASSES = K // (P * PACK)
WORD_TILES = K // 2 // P
TILES = TOKENS // P
UNITS = BATCH * TILES
PAIR_BLOCKS = HEADS * HEADS // P
HEADS_PER_BLOCK = HEADS // PAIR_BLOCKS
D_ON_GPSIMD = 2
D_ON_VECTOR = HD - D_ON_GPSIMD

LOAD_AHEAD = 4
QUANTISE_LAG = 1
PROJECT_LAG = QUANTISE_LAG + 1
MULTIPLY_LAG = PROJECT_LAG + 1
SUM_LAG = MULTIPLY_LAG + 1
BACK_LAG = SUM_LAG + 1
SHIFT_LAG = BACK_LAG + 1
NORMALISE_LAG = SHIFT_LAG + 1

FLOPS = 2 * BATCH * TOKENS * K * QK_COLS + 2 * BATCH * TOKENS * HEADS * HEADS * HD


def tile_attention_pa_t_kernel(tc, x, w_qk, b_qk, out):
    nc = tc.nc
    with ExitStack() as stack:
        stack.enter_context(tc.manual_schedule())
        const = stack.enter_context(tc.tile_pool(name="const", bufs=1))
        x_pool = stack.enter_context(tc.tile_pool(name="x_pool", bufs=LOAD_AHEAD + 1))
        work = stack.enter_context(tc.tile_pool(name="work", bufs=2))
        soft_pool = stack.enter_context(tc.tile_pool(name="soft_pool", bufs=3))
        gpsimd_pool = stack.enter_context(tc.tile_pool(name="gpsimd_pool", bufs=1))
        psum_xt = stack.enter_context(tc.psum_pool(name="psum_xt", bufs=2))
        psum_qk = stack.enter_context(tc.psum_pool(name="psum_qk", bufs=2))
        psum_sum = stack.enter_context(tc.psum_pool(name="psum_sum", bufs=2))
        psum_back = stack.enter_context(tc.psum_pool(name="psum_back", bufs=2))

        x_rows_of = {}
        x_grouped_of = {}
        x_mx_of = {}
        qk_sum_of = {}
        qk_of = {}
        products_of = {}
        last_products_of = {}
        pair_rows_of = {}
        pair_rows_kept_of = {}
        score_of = {}
        top_of = {}
        shift_of = {}
        prob_of = {}
        total_of = {}
        inverse_of = {}

        def load_x(unit):
            n, j = divmod(unit, TILES)
            x_rows = x_pool.tile([P, K], BF16)
            nc.sync.dma_start(out=x_rows[:], in_=x[n].rearrange("(t j) k -> t j k", j=TILES)[:, j, :])
            x_rows_of[unit] = x_rows

        load_x(0)

        ident = const.tile([P, P], F32)
        make_identity(nc, ident[:])

        w_codes = const.tile([P, PASSES, QK_COLS], U32, align_bytes=64)
        w_scales = const.tile([P, PASSES, QK_COLS], U8, align_bytes=64)
        for c in range(PASSES):
            w_rows = const.tile([P, PACK, QK_COLS], BF16, name="w_rows%d" % c)
            for u in range(2):
                first = (2 * c + u) * 2 * P
                nc.sync.dma_start(
                    out=w_rows[:, 2 * u : 2 * u + 2, :],
                    in_=w_qk[first : first + 2 * P, :].rearrange("(p e) n -> p e n", e=2),
                )
            w_grouped = const.tile([P, QK_COLS, PACK], BF16, align_bytes=64, name="w_grouped%d" % c)
            for half in range(2):
                cols = slice(half * Q_COLS, (half + 1) * Q_COLS)
                nc.vector.tensor_copy(
                    out=w_grouped[:, cols, :].rearrange("p (d h) v -> p d h v", d=HD),
                    in_=w_rows[:, :, cols].rearrange("p v (h d) -> p d h v", d=HD),
                )
            nc.vector.quantize_mx(
                out=w_codes[:, c, :].bitcast(FP8X4),
                scales=w_scales[:, c, :],
                in_=w_grouped[:].rearrange("p n v -> p (n v)"),
            )

        bias_bf16 = const.tile([P, QK_COLS], BF16)
        nc.sync.dma_start(out=bias_bf16[:], in_=b_qk.partition_broadcast(P))
        bias = const.tile([P, QK_COLS], F32)
        nc.vector.tensor_copy(
            out=bias[:].rearrange("p (c d h) -> p c d h", c=2, d=HD),
            in_=bias_bf16[:].rearrange("p (c h d) -> p c d h", c=2, d=HD),
        )

        for unit in range(1, LOAD_AHEAD):
            load_x(unit)

        def turn_x(unit):
            x_words = x_rows_of[unit][:].bitcast(F32)
            x_turned = psum_xt.tile([P, WORD_TILES, P], F32)
            for w in range(WORD_TILES):
                nc.tensor.transpose(x_turned[:, w, :], x_words[:, w * P : (w + 1) * P], ident[:])
            x_grouped = work.tile([P, K], BF16, align_bytes=64)
            nc.scalar.copy(
                out=x_grouped[:].bitcast(F32).rearrange("p (c t u) -> p c t u", c=PASSES, u=2),
                in_=x_turned[:].rearrange("p (c u) t -> p c t u", u=2),
            )
            x_grouped_of[unit] = x_grouped

        def quantise_x(unit):
            x_codes = work.tile([P, PASSES, P], U32, align_bytes=64)
            x_scales = work.tile([P, PASSES, P], U8, align_bytes=64)
            nc.vector.quantize_mx(
                out=x_codes[:].rearrange("p c t -> p (c t)").bitcast(FP8X4),
                scales=x_scales[:].rearrange("p c t -> p (c t)"),
                in_=x_grouped_of[unit][:],
            )
            x_mx_of[unit] = (x_codes, x_scales)

        def project(unit):
            x_codes, x_scales = x_mx_of[unit]
            qk_sum = psum_qk.tile([P, QK_COLS], F32)
            for c in range(PASSES):
                nc.tensor.matmul_mx(
                    out=qk_sum[:],
                    lhsT=x_codes[:, c, :].bitcast(FP8X4),
                    lhsT_scale=x_scales[:, c, :],
                    rhs=w_codes[:, c, :].bitcast(FP8X4),
                    rhs_scale=w_scales[:, c, :],
                    start=(c == 0),
                    stop=(c == PASSES - 1),
                )
            qk_sum_of[unit] = qk_sum

        def add_bias(unit):
            qk = work.tile([P, QK_COLS], F32)
            nc.vector.tensor_tensor(out=qk[:], in0=qk_sum_of[unit][:], in1=bias[:], op=ALU.add)
            qk_of[unit] = qk

        def multiply(engine, products, qk, d0, d1):
            shape = [P, d1 - d0, HEADS, HEADS]
            engine.tensor_tensor(
                out=products[:],
                in0=qk[:, 0:Q_COLS]
                .rearrange("p (d h) -> p d h", d=HD)[:, d0:d1, :]
                .unsqueeze(3)
                .to_broadcast(shape),
                in1=qk[:, Q_COLS:QK_COLS]
                .rearrange("p (d g) -> p d g", d=HD)[:, d0:d1, :]
                .unsqueeze(2)
                .to_broadcast(shape),
                op=ALU.mult,
            )

        def multiply_heads(unit):
            products = work.tile([P, D_ON_VECTOR, HEADS, HEADS], F32)
            multiply(nc.vector, products, qk_of[unit], 0, D_ON_VECTOR)
            products_of[unit] = products

        def multiply_last_d(unit):
            last_products = gpsimd_pool.tile([P, D_ON_GPSIMD, HEADS, HEADS], F32)
            multiply(nc.gpsimd, last_products, qk_of[unit], D_ON_VECTOR, HD)
            last_products_of[unit] = last_products

        def sum_over_d(unit):
            pair_rows = psum_sum.tile([P, PAIR_BLOCKS, P], F32)
            for b in range(PAIR_BLOCKS):
                h0 = b * HEADS_PER_BLOCK
                for d in range(HD):
                    if d < D_ON_VECTOR:
                        of_d = products_of[unit][:, d, :, :]
                    else:
                        of_d = last_products_of[unit][:, d - D_ON_VECTOR, :, :]
                    nc.tensor.matmul(
                        out=pair_rows[:, b, :],
                        lhsT=of_d[:, h0 : h0 + HEADS_PER_BLOCK, :].rearrange("p h g -> p (h g)"),
                        rhs=ident[:],
                        is_transpose=True,
                        start=(d == 0),
                        stop=(d == HD - 1),
                    )
            pair_rows_of[unit] = pair_rows

        def keep_pair_rows(unit):
            pair_rows_kept = work.tile([P, PAIR_BLOCKS, P], F32)
            nc.scalar.copy(out=pair_rows_kept[:], in_=pair_rows_of[unit][:])
            pair_rows_kept_of[unit] = pair_rows_kept

        def turn_back(unit):
            score = psum_back.tile([P, HEADS, HEADS], F32)
            for b in range(PAIR_BLOCKS):
                h0 = b * HEADS_PER_BLOCK
                nc.tensor.transpose(
                    score[:, h0 : h0 + HEADS_PER_BLOCK, :].rearrange("p h g -> p (h g)"),
                    pair_rows_kept_of[unit][:, b, :],
                    ident[:],
                )
            score_of[unit] = score

        def find_top(unit):
            top = soft_pool.tile([P, HEADS], F32)
            nc.vector.tensor_reduce(out=top[:], in_=score_of[unit][:], axis=AXIS.X, op=ALU.max)
            top_of[unit] = top

        def negate_top(unit):
            shift = soft_pool.tile([P, HEADS], F32)
            nc.vector.tensor_scalar(
                out=shift[:], in0=top_of[unit][:], scalar1=-(HD**-0.5), scalar2=None, op0=ALU.mult
            )
            shift_of[unit] = shift

        def exponential(unit):
            prob = soft_pool.tile([P, HEADS, HEADS], F32)
            total = soft_pool.tile([P, HEADS], F32)
            for h in range(HEADS):
                nc.scalar.activation(
                    out=prob[:, h, :],
                    in_=score_of[unit][:, h, :],
                    func=ACT.Exp,
                    bias=shift_of[unit][:, h : h + 1],
                    scale=HD**-0.5,
                    accum_out=total[:, h : h + 1],
                )
            prob_of[unit] = prob
            total_of[unit] = total

        def invert(unit):
            inverse = soft_pool.tile([P, HEADS], F32)
            nc.vector.reciprocal(out=inverse[:], in_=total_of[unit][:])
            inverse_of[unit] = inverse

        def scale_and_store(unit):
            n, j = divmod(unit, TILES)
            prob = prob_of[unit]
            for h in range(HEADS):
                nc.scalar.activation(
                    out=prob[:, h, :],
                    in_=prob[:, h, :],
                    func=ACT.Copy,
                    scale=inverse_of[unit][:, h : h + 1],
                )
            nc.sync.dma_start(
                out=out[n].rearrange("(t j) h g -> t j (h g)", j=TILES)[:, j, :],
                in_=prob[:].rearrange("p h g -> p (h g)"),
            )

        def run(stage, unit):
            if 0 <= unit < UNITS:
                stage(unit)

        for step in range(UNITS + NORMALISE_LAG):
            run(load_x, step + LOAD_AHEAD)
            run(multiply_last_d, step - SUM_LAG)
            run(keep_pair_rows, step - BACK_LAG)
            run(project, step - PROJECT_LAG)
            run(find_top, step - SHIFT_LAG)
            run(add_bias, step - MULTIPLY_LAG)
            run(negate_top, step - SHIFT_LAG)
            run(exponential, step - SHIFT_LAG)
            run(invert, step - NORMALISE_LAG)
            run(quantise_x, step - QUANTISE_LAG)
            run(multiply_heads, step - MULTIPLY_LAG)
            run(turn_x, step)
            run(scale_and_store, step - NORMALISE_LAG)
            run(sum_over_d, step - SUM_LAG)
            run(turn_back, step - BACK_LAG)
